import numpy as np
import ml_dtypes


def mxq(x, axis, fmt="e4m3"):
    dtype, down = {"e4m3": (ml_dtypes.float8_e4m3fn, 7), "e5m2": (ml_dtypes.float8_e5m2, 14)}[fmt]
    v = np.moveaxis(np.asarray(x, np.float32).astype(ml_dtypes.bfloat16).astype(np.float64), axis, -1)
    blocks = v.reshape(v.shape[:-1] + (-1, 32))
    amax = np.abs(blocks).max(-1, keepdims=True)
    byte = np.maximum(np.where(amax > 0, np.frexp(amax)[1] - 1 + 127, 0) - down, 1)
    scale = np.exp2(byte - 127.0)
    codes = (blocks / scale).astype(np.float32).astype(dtype).astype(np.float64)
    return np.moveaxis((codes * scale).reshape(v.shape), -1, axis)


WIDE = False


def mx_kscale(k):
    if not WIDE:
        return np.ones(k)
    levels = np.array([18, -18])
    if k % 512:
        return np.exp2(np.random.permutation(np.resize(levels, k // 32))).repeat(32)
    a = np.empty((k // 512, 16))
    for p in range(k // 512):
        a[p, :8] = np.random.permutation(np.resize(levels, 8))
        for g in range(8):
            far = levels[np.abs(levels - a[p, g]) >= 10]
            a[p, g + 8] = far[np.random.randint(len(far))]
    return np.exp2(a.ravel()).repeat(32)


BF16 = ml_dtypes.bfloat16


def bf(x):
    return np.asarray(x, np.float32).astype(BF16)


def f64(x):
    return np.asarray(x).astype(np.float64)


B, N, DIN, DS, GE, HID, NS, KC = 1, 1024, 128, 256, 8, 32, 2, 2
DO = DS
C = DIN + DS + DS
F = NS * KC * C
SHARP = 4.0


def sigmoid(v):
    return 1.0 / (1.0 + np.exp(-v))


def softmax(v):
    e = np.exp(v - v.max(-1, keepdims=True))
    return e / e.sum(-1, keepdims=True)


def setup_inputs():
    s = mx_kscale(N)
    u = mx_kscale(NS * N)
    v = mx_kscale(2 * DO)
    adj = bf(softmax(SHARP * np.random.standard_normal((NS, B, N, N))))
    xg0 = bf(np.random.standard_normal((B, N, F)) * 0.8)
    w0 = bf(np.random.standard_normal((F, DO + DO)) * 1.5 / np.sqrt(F))
    b0 = bf(np.random.standard_normal(DO + DO) * 0.5)
    xt = bf(np.random.standard_normal((B, N, DIN)))
    state1 = bf(np.random.standard_normal((B, N, DS)))
    state2 = bf(np.random.standard_normal((B, N, DS)))
    z = sigmoid(f64(xg0) @ f64(w0) + f64(b0))
    gf = np.ones((N, NS, KC, C))
    gf[:, :, 0] /= s[:, None, None]
    gf[:, :, 1] *= u.reshape(NS, N).T[:, :, None]
    gf[..., DIN:] *= v
    g = np.random.standard_normal((B, N, F)) * np.exp2(np.random.randint(-6, 1, (B, N, 1))) * 4.0 * gf.reshape(1, N, F)
    return {"xg_gate": bf(f64(xg0) * s[:, None]),
            "gate_w_z": bf(f64(w0) / v),
            "gate_b_z": b0,
            "xt": xt,
            "state1": state1,
            "state2": state2,
            "supports": bf(f64(adj) / u.reshape(NS, 1, N, 1) / s),
            "z": np.asarray(z, np.float32),
            "grad_out": bf(g)}


def reference(xg_gate, gate_w_z, gate_b_z, xt, state1, state2, supports, z, grad_out):
    g = f64(grad_out).reshape(N, NS, KC, C)[..., DIN:]
    g1 = np.transpose(g[:, :, 1], (1, 0, 2)).reshape(NS * N, 2 * DO)
    a = f64(supports).reshape(NS * N, N)
    dh = mxq(a, 0, "e4m3").T @ mxq(g1, 0, "e5m2")
    dh = dh + g[:, :, 0].sum(1)
    st = np.concatenate([f64(state1)[0], f64(state2)[0]], axis=-1)
    zf = f64(z)[0]
    dz = dh * st * (zf * (1.0 - zf))
    dxg = mxq(dz, 1, "e5m2") @ mxq(f64(gate_w_z), 1, "e4m3").T
    dw = mxq(f64(xg_gate)[0], 0, "e4m3").T @ mxq(dz, 0, "e5m2")
    return dxg.reshape(B, N, F), dw

@@ -1,0 +1,331 @@
+from contextlib import ExitStack
+
+import concourse.mybir as mybir
+from concourse.masks import make_identity
+
+N, F, D = 1024, 2560, 512
+DS = 256
+DIN = 128
+TERM = 640
+NS = 2
+
+FLOPS = 2 * (NS * N * N * D + 2 * N * D * F)
+BYTES = 2 * (N * F + F * D + N * D + NS * N * N + 4 * N * D) + 4 * (N * D + N * F + F * D)
+
+F32 = mybir.dt.float32
+BF16 = mybir.dt.bfloat16
+U32 = mybir.dt.uint32
+U8 = mybir.dt.uint8
+E4M3 = mybir.dt.float8_e4m3fn_x4
+E5M2 = mybir.dt.float8_e5m2_x4
+ALU = mybir.AluOpType
+
+P = 128
+PACK = 4
+KP = P * PACK
+UNIT = KP * PACK
+HALVES = N // KP
+CHUNKS = F // KP
+
+
+def tile_dgggl_pa_v_kernel(tc, xg_gate, gate_w_z, gate_b_z, xt, state1, state2, supports, z, grad_out,
+                                        out_0, out_1):
+    nc = tc.nc
+    with ExitStack() as ctx:
+        sb = ctx.enter_context(tc.tile_pool(name="sb", bufs=1))
+        ps = ctx.enter_context(tc.psum_pool(name="ps", bufs=1))
+
+        ident = sb.tile([P, P], F32, name="ident")
+        make_identity(nc, ident[:])
+        ctx.enter_context(tc.manual_schedule())
+
+        def slot(tag, width, dtype):
+            return sb.tile([P, width], dtype, name=tag, tag=tag, align_bytes=64)
+
+        def bank(b):
+            return ps.tile([P, KP], F32, name="bank%d" % b, tag="bank%d" % b)
+
+        def copy(on_vector, out, in_):
+            if on_vector:
+                nc.vector.tensor_copy(out=out, in_=in_)
+            else:
+                nc.scalar.copy(out=out, in_=in_)
+
+        def grouped_tile():
+            return sb.tile([P, UNIT], BF16, name="grouped", tag="grouped", bufs=6, align_bytes=64)
+
+        def interleave(on_vector, rows):
+            grouped = grouped_tile()
+            copy(on_vector, grouped[:].rearrange("p (c i j) -> p c j i", i=PACK, j=PACK),
+                 rows.rearrange("p j (c i) -> p c j i", i=PACK))
+            return grouped
+
+        def interleave_sorted(on_vector, rows):
+            grouped = grouped_tile()
+            copy(on_vector, grouped[:].rearrange("p (t a b j) -> p a t b j", t=PACK, b=2, j=PACK),
+                 rows.rearrange("p j (a b t) -> p a t b j", b=2, t=PACK))
+            return grouped
+
+        def quantize(grouped, index, fmt):
+            codes = slot("codes%d" % index, KP, U32)
+            scales = slot("scales%d" % index, KP, U8)
+            nc.vector.quantize_mx(out=codes[:].bitcast(fmt), scales=scales[:], in_=grouped[:])
+            return codes, scales, fmt
+
+        def multiply(acc, stationary, tile, moving, start, stop):
+            cols = slice(tile * P, (tile + 1) * P)
+            nc.tensor.matmul_mx(out=acc[:], lhsT=stationary[0][:, cols].bitcast(stationary[2]),
+                                lhsT_scale=stationary[1][:, cols], rhs=moving[0][:].bitcast(moving[2]),
+                                rhs_scale=moving[1][:], start=start, stop=stop)
+
+        def by_node(ap, h):
+            return ap[h * KP:(h + 1) * KP, :].rearrange("(p j) w -> p j w", j=PACK)
+
+        def load(tile_ap, src):
+            nc.sync.dma_start(out=tile_ap, in_=src)
+
+        g_raw = [slot("stage0", 2 * UNIT, BF16), slot("stage1", 2 * UNIT, BF16)]
+        a_raw = [slot("wide0", 4 * UNIT, BF16), slot("wide1", 4 * UNIT, BF16)]
+        g_rows, a_rows = [], []
+        for q in range(NS * HALVES):
+            s, h = divmod(q, HALVES)
+            g_rows.append(g_raw[s][:].rearrange("p (h j w) -> p h j w", h=HALVES, j=PACK)[:, h, :, :])
+            a_rows.append(a_raw[s][:].rearrange("p (h j w) -> p h j w", h=HALVES, j=PACK)[:, h, :, :])
+
+        direct = grad_out[0, :, :].rearrange("n (s x) -> (n s) x", s=NS)
+        p_raw, z_sb, st_sb = {}, {}, {}
+
+        def load_g(q):
+            s, h = divmod(q, HALVES)
+            first = (2 * s + 1) * TERM + DIN
+            load(g_rows[q], by_node(grad_out[0, :, :][:, first:first + D], h))
+
+        def load_a(q):
+            s, h = divmod(q, HALVES)
+            load(a_rows[q], by_node(supports[s, 0, :, :], h))
+
+        def load_direct(h):
+            p_raw[h] = slot("stage%d" % (2 + 2 * h), 2 * UNIT, BF16)
+            load(p_raw[h][:].rearrange("p (r c) -> p r c", c=D),
+                 direct[h * NS * KP:(h + 1) * NS * KP, DIN:DIN + D].rearrange("(p r) c -> p r c", r=PACK * NS))
+
+        def load_gate(h):
+            z_sb[h] = slot("stage%d" % (3 + 2 * h), UNIT, F32)
+            st_sb[h] = slot("state%d" % h, UNIT, BF16)
+            load(z_sb[h][:].rearrange("p (j w) -> p j w", j=PACK), by_node(z[0, :, :], h))
+            for s, state in enumerate((state1, state2)):
+                load(st_sb[h][:].rearrange("p (s j c) -> p s j c", s=2, j=PACK)[:, s, :, :], by_node(state[0, :, :], h))
+
+        for q in range(NS * HALVES):
+            load_g(q)
+            load_a(q)
+            if q == 1:
+                load_gate(0)
+            if q == 2:
+                load_direct(0)
+        w_words = []
+        for tag, first, count in (("stage6", 0, 2), ("stage7", 2, 2), ("w_last", 4, 1)):
+            w_raw = slot(tag, count * UNIT, BF16)
+            load(w_raw[:].rearrange("p (g x) -> p g x", g=count),
+                 gate_w_z[first * KP:(first + count) * KP, :].rearrange("(g p j) k -> p g (j k)", p=P, j=PACK))
+            for g in range(count):
+                w_words.append(w_raw[:].bitcast(F32).rearrange("p (g j x) -> p g j x", g=count, j=PACK)[:, g, :, :])
+        load_direct(1)
+        load_gate(1)
+
+        dh = {}
+        g_mx, a_mx, staged = {}, {}, {}
+
+        def copy_g(q, on_vector):
+            staged["g", q] = interleave(on_vector, g_rows[q])
+
+        def copy_a(q, h, on_vector):
+            staged["a", q, h] = interleave_sorted(on_vector, a_rows[q][:, :, h * KP:(h + 1) * KP])
+
+        def quant_g(q):
+            g_mx[q] = quantize(staged["g", q], 8 + q, E5M2)
+
+        def quant_a(q, h):
+            a_mx[q, h] = quantize(staged["a", q, h], 2 * q + h, E4M3)
+
+        def dh_pass(q, h):
+            if q == 0:
+                dh[h] = [bank(PACK * h + t) for t in range(PACK)]
+            for t in range(PACK):
+                multiply(dh[h][t], a_mx[q, h], t, g_mx[q], q == 0, q == NS * HALVES - 1)
+
+        d_sb, dz_sb = {}, {}
+
+        def add_direct(h):
+            d_sb[h] = slot("d%d" % h, UNIT, F32)
+            terms = p_raw[h][:].rearrange("p (j s c) -> p j s c", j=PACK, s=NS)
+            nc.vector.tensor_tensor(out=d_sb[h][:].rearrange("p (j c) -> p j c", j=PACK),
+                                    in0=terms[:, :, 0, :], in1=terms[:, :, 1, :], op=ALU.add)
+
+        def gate_slope(h):
+            nc.vector.scalar_tensor_tensor(out=z_sb[h][:], in0=z_sb[h][:], scalar=1.0, in1=z_sb[h][:],
+                                           op0=ALU.subtract, op1=ALU.mult)
+
+        def add_product(h):
+            for t in range(PACK):
+                part = d_sb[h][:, t * D:(t + 1) * D]
+                nc.vector.tensor_tensor(out=part, in0=dh[h][t][:], in1=part, op=ALU.add)
+
+        def times_state(h):
+            factor = z_sb[h][:].rearrange("p (j s c) -> p j s c", j=PACK, s=2)
+            nc.vector.tensor_tensor(out=factor, in0=factor,
+                                    in1=st_sb[h][:].rearrange("p (s j c) -> p j s c", s=2, j=PACK), op=ALU.mult)
+
+        def round_dz(h):
+            dz_sb[h] = slot("dz%d" % h, UNIT, BF16)
+            nc.vector.scalar_tensor_tensor(out=dz_sb[h][:], in0=d_sb[h][:], scalar=-1.0, in1=z_sb[h][:],
+                                           op0=ALU.mult, op1=ALU.mult)
+
+        copy_g(0, True)
+        quant_g(0)
+        copy_a(0, 0, False)
+        copy_g(1, True)
+        quant_a(0, 0)
+        dh_pass(0, 0)
+        copy_a(0, 1, False)
+        copy_a(1, 0, True)
+        quant_g(1)
+        quant_a(0, 1)
+        dh_pass(0, 1)
+        copy_a(1, 1, False)
+        quant_a(1, 0)
+        dh_pass(1, 0)
+        gate_slope(0)
+        copy_g(2, False)
+        quant_a(1, 1)
+        dh_pass(1, 1)
+        times_state(0)
+        copy_a(2, 0, False)
+        quant_g(2)
+        add_direct(0)
+        copy_g(3, False)
+        quant_a(2, 0)
+        dh_pass(2, 0)
+        copy_a(2, 1, False)
+        copy_a(3, 0, True)
+        quant_g(3)
+        quant_a(3, 0)
+        dh_pass(3, 0)
+        copy_a(3, 1, False)
+
+        x_rows = []
+        for h in range(HALVES):
+            x_raw = slot("wide%d" % h, PACK * F, BF16)
+            x_rows.append(x_raw[:].rearrange("p (j w) -> p j w", j=PACK))
+            load(x_rows[h], by_node(xg_gate[0, :, :], h))
+
+        def transpose_pairs(words, banks, order):
+            grouped = grouped_tile()
+            for b in range(2):
+                turned = bank(banks[b])
+                for r in range(2):
+                    for u in range(2):
+                        k = 2 * r + u
+                        nc.tensor.transpose(turned[:, k * P:(k + 1) * P], words[:, 2 * b + r, u:2 * P:2], ident[:])
+                if order == "rows":
+                    dst = grouped[:].bitcast(F32).rearrange("q (p j u) -> q p j u", j=PACK, u=2)[:, :, 2 * b:2 * b + 2, :]
+                    src = turned[:].rearrange("q (j u p) -> q p j u", j=2, u=2)
+                else:
+                    dst = grouped[:].bitcast(F32).rearrange("q (j p u) -> q j p u", j=PACK, u=2)[:, 2 * b:2 * b + 2, :, :]
+                    src = turned[:].rearrange("q (j u p) -> q j p u", j=2, u=2)
+                nc.scalar.copy(out=dst, in_=src)
+            return grouped
+
+        w_mx, dzf_mx, dzn_mx, x_mx = {}, {}, {}, {}
+
+        def turn_w(g):
+            staged["w", g] = transpose_pairs(w_words[g], (2 * (g % 2), 2 * (g % 2) + 1), "rows")
+
+        def quant_w(g):
+            w_mx[g] = quantize(staged["w", g], 12 + g, E4M3)
+
+        def turn_dz(h, banks):
+            words = dz_sb[h][:].bitcast(F32).rearrange("p (j x) -> p j x", j=PACK)
+            staged["dzf", h] = transpose_pairs(words, banks, "tiles")
+
+        def quant_dzf(h):
+            dzf_mx[h] = quantize(staged["dzf", h], 8 + h, E5M2)
+
+        def copy_dzn(h):
+            staged["dzn", h] = interleave(True, dz_sb[h][:].rearrange("p (j w) -> p j w", j=PACK))
+
+        def quant_dzn(h):
+            dzn_mx[h] = quantize(staged["dzn", h], 10 + h, E5M2)
+
+        def copy_x(c, h):
+            staged["x", c, h] = interleave(True, x_rows[h][:, :, c * KP:(c + 1) * KP])
+
+        def quant_x(c, h):
+            index = 2 * c + h
+            x_mx[c, h] = quantize(staged["x", c, h], index if index < 8 else index + 9, E4M3)
+
+        stage_order = (0, 1, 2, 3, 6, 7, 4, 5)
+
+        def out0_tile(h, t, banks):
+            result = slot("stage%d" % stage_order[PACK * h + t], F, F32)
+            for g in range(CHUNKS):
+                acc = bank(banks[(CHUNKS * t + g) % len(banks)])
+                multiply(acc, dzf_mx[h], t, w_mx[g], True, True)
+                nc.scalar.copy(out=result[:, g * KP:(g + 1) * KP], in_=acc[:])
+            nc.sync.dma_start(out=by_node(out_0[0, :, :], h)[:, t, :], in_=result[:])
+
+        def out1_chunk(c, vector_tiles):
+            result = slot("stage%d" % stage_order[c], UNIT, F32)
+            for i in range(PACK):
+                acc = bank((PACK * c + i) % 8)
+                for h in range(HALVES):
+                    multiply(acc, x_mx[c, h], i, dzn_mx[h], h == 0, h == HALVES - 1)
+                copy(i in vector_tiles, result[:, i * D:(i + 1) * D], acc[:])
+            nc.sync.dma_start(out=out_1[c * KP:(c + 1) * KP, :].rearrange("(i p) n -> p i n", p=P),
+                              in_=result[:].rearrange("p (i n) -> p i n", i=PACK))
+
+        add_product(0)
+        turn_w(0)
+        turn_w(1)
+        quant_a(2, 1)
+        round_dz(0)
+        dh_pass(2, 1)
+        quant_a(3, 1)
+        turn_w(2)
+        quant_w(0)
+        turn_w(3)
+        quant_w(1)
+        turn_w(4)
+        turn_dz(0, (2, 3))
+        dh_pass(3, 1)
+        quant_w(2)
+        quant_w(3)
+        quant_w(4)
+        quant_dzf(0)
+
+        for t in range(PACK):
+            out0_tile(0, t, (0, 1, 2, 3))
+
+        add_direct(1)
+        gate_slope(1)
+        add_product(1)
+        times_state(1)
+        round_dz(1)
+        turn_dz(1, (4, 5))
+        copy_dzn(0)
+        quant_dzf(1)
+
+        for t in range(PACK):
+            out0_tile(1, t, (6, 7, 0, 1, 2, 3, 4, 5))
+
+        copy_dzn(1)
+        quant_dzn(0)
+        copy_x(0, 0)
+        quant_dzn(1)
+        for c in range(CHUNKS):
+            copy_x(c, 1)
+            quant_x(c, 0)
+            if c + 1 < CHUNKS:
+                copy_x(c + 1, 0)
+            quant_x(c, 1)
+            out1_chunk(c, (1, 3) if c == CHUNKS - 1 else ())

@@ -37,6 +37,8 @@ def tile_dgggl_pa_v_kernel(tc, xg_gate, gate_w_z, gate_b_z, xt, state1, state2, 
 
         ident = sb.tile([P, P], F32, name="ident")
         make_identity(nc, ident[:])
+        ident_bf = sb.tile([P, P], BF16, name="ident_bf")
+        make_identity(nc, ident_bf[:])
         ctx.enter_context(tc.manual_schedule())
 
         def slot(tag, width, dtype):
@@ -58,12 +60,6 @@ def tile_dgggl_pa_v_kernel(tc, xg_gate, gate_w_z, gate_b_z, xt, state1, state2, 
             grouped = grouped_tile()
             copy(on_vector, grouped[:].rearrange("p (c i j) -> p c j i", i=PACK, j=PACK),
                  rows.rearrange("p j (c i) -> p c j i", i=PACK))
-            return grouped
-
-        def interleave_sorted(on_vector, rows):
-            grouped = grouped_tile()
-            copy(on_vector, grouped[:].rearrange("p (t a b j) -> p a t b j", t=PACK, b=2, j=PACK),
-                 rows.rearrange("p j (a b t) -> p a t b j", b=2, t=PACK))
             return grouped
 
         def quantize(grouped, index, fmt):
@@ -116,22 +112,29 @@ def tile_dgggl_pa_v_kernel(tc, xg_gate, gate_w_z, gate_b_z, xt, state1, state2, 
             for s, state in enumerate((state1, state2)):
                 load(st_sb[h][:].rearrange("p (s j c) -> p s j c", s=2, j=PACK)[:, s, :, :], by_node(state[0, :, :], h))
 
-        for q in range(NS * HALVES):
-            load_g(q)
-            load_a(q)
-            if q == 1:
-                load_gate(0)
-            if q == 2:
-                load_direct(0)
         w_words = []
-        for tag, first, count in (("stage6", 0, 2), ("stage7", 2, 2), ("w_last", 4, 1)):
+
+        def load_w(tag, first, count):
             w_raw = slot(tag, count * UNIT, BF16)
             load(w_raw[:].rearrange("p (g x) -> p g x", g=count),
                  gate_w_z[first * KP:(first + count) * KP, :].rearrange("(g p j) k -> p g (j k)", p=P, j=PACK))
             for g in range(count):
                 w_words.append(w_raw[:].bitcast(F32).rearrange("p (g j x) -> p g j x", g=count, j=PACK)[:, g, :, :])
+
+        load_g(0)
+        load_a(0)
+        load_g(1)
+        load_a(1)
+        load_g(2)
+        load_a(2)
+        load_g(3)
+        load_a(3)
+        load_direct(0)
+        load_gate(0)
+        load_w("stage6", 0, 2)
         load_direct(1)
         load_gate(1)
+        load_w("w_last", 2, 3)
 
         dh = {}
         g_mx, a_mx, staged = {}, {}, {}
@@ -140,7 +143,7 @@ def tile_dgggl_pa_v_kernel(tc, xg_gate, gate_w_z, gate_b_z, xt, state1, state2, 
             staged["g", q] = interleave(on_vector, g_rows[q])
 
         def copy_a(q, h, on_vector):
-            staged["a", q, h] = interleave_sorted(on_vector, a_rows[q][:, :, h * KP:(h + 1) * KP])
+            staged["a", q, h] = interleave(on_vector, a_rows[q][:, :, h * KP:(h + 1) * KP])
 
         def quant_g(q):
             g_mx[q] = quantize(staged["g", q], 8 + q, E5M2)
@@ -152,74 +155,54 @@ def tile_dgggl_pa_v_kernel(tc, xg_gate, gate_w_z, gate_b_z, xt, state1, state2, 
             if q == 0:
                 dh[h] = [bank(PACK * h + t) for t in range(PACK)]
             for t in range(PACK):
-                multiply(dh[h][t], a_mx[q, h], t, g_mx[q], q == 0, q == NS * HALVES - 1)
+                multiply(dh[h][t], g_mx[q], t, a_mx[q, h], q == 0, q == NS * HALVES - 1)
 
-        d_sb, dz_sb = {}, {}
+        d_sb, total, dz_sb = {}, {}, {}
 
-        def add_direct(h):
+        def empty_dh(h, on_vector):
             d_sb[h] = slot("d%d" % h, UNIT, F32)
+            for f in range(PACK):
+                copy(on_vector, d_sb[h][:, f * KP:(f + 1) * KP].rearrange("q (t p) -> q t p", t=PACK),
+                     dh[h][f][:].rearrange("q (p t) -> q t p", t=PACK))
+
+        def add_product(h, t, b):
+            total[h, t] = bank(b)
+            for f in range(PACK):
+                first = f * KP + t * P
+                nc.tensor.matmul(out=total[h, t][:, f * P:(f + 1) * P], lhsT=d_sb[h][:, first:first + P],
+                                 rhs=ident[:], start=f == 0, stop=False, is_transpose=True)
+
+        def add_direct(h, t):
             terms = p_raw[h][:].rearrange("p (j s c) -> p j s c", j=PACK, s=NS)
-            nc.vector.tensor_tensor(out=d_sb[h][:].rearrange("p (j c) -> p j c", j=PACK),
-                                    in0=terms[:, :, 0, :], in1=terms[:, :, 1, :], op=ALU.add)
+            for s in range(NS):
+                nc.tensor.matmul(out=total[h, t][:], lhsT=ident_bf[:], rhs=terms[:, t, s, :], start=False,
+                                 stop=s == NS - 1)
 
         def gate_slope(h):
             nc.vector.scalar_tensor_tensor(out=z_sb[h][:], in0=z_sb[h][:], scalar=1.0, in1=z_sb[h][:],
                                            op0=ALU.subtract, op1=ALU.mult)
-
-        def add_product(h):
-            for t in range(PACK):
-                part = d_sb[h][:, t * D:(t + 1) * D]
-                nc.vector.tensor_tensor(out=part, in0=dh[h][t][:], in1=part, op=ALU.add)
 
         def times_state(h):
             factor = z_sb[h][:].rearrange("p (j s c) -> p j s c", j=PACK, s=2)
             nc.vector.tensor_tensor(out=factor, in0=factor,
                                     in1=st_sb[h][:].rearrange("p (s j c) -> p j s c", s=2, j=PACK), op=ALU.mult)
 
-        def round_dz(h):
-            dz_sb[h] = slot("dz%d" % h, UNIT, BF16)
-            nc.vector.scalar_tensor_tensor(out=dz_sb[h][:], in0=d_sb[h][:], scalar=-1.0, in1=z_sb[h][:],
-                                           op0=ALU.mult, op1=ALU.mult)
+        def round_dz(h, t):
+            if t == 0:
+                dz_sb[h] = slot("dz%d" % h, UNIT, BF16)
+            cols = slice(t * D, (t + 1) * D)
+            nc.vector.scalar_tensor_tensor(out=dz_sb[h][:, cols], in0=total[h, t][:], scalar=-1.0,
+                                           in1=z_sb[h][:, cols], op0=ALU.mult, op1=ALU.mult)
 
-        copy_g(0, True)
-        quant_g(0)
-        copy_a(0, 0, False)
-        copy_g(1, True)
-        quant_a(0, 0)
-        dh_pass(0, 0)
-        copy_a(0, 1, False)
-        copy_a(1, 0, True)
-        quant_g(1)
-        quant_a(0, 1)
-        dh_pass(0, 1)
-        copy_a(1, 1, False)
-        quant_a(1, 0)
-        dh_pass(1, 0)
-        gate_slope(0)
-        copy_g(2, False)
-        quant_a(1, 1)
-        dh_pass(1, 1)
-        times_state(0)
-        copy_a(2, 0, False)
-        quant_g(2)
-        add_direct(0)
-        copy_g(3, False)
-        quant_a(2, 0)
-        dh_pass(2, 0)
-        copy_a(2, 1, False)
-        copy_a(3, 0, True)
-        quant_g(3)
-        quant_a(3, 0)
-        dh_pass(3, 0)
-        copy_a(3, 1, False)
 
-        x_rows = []
-        for h in range(HALVES):
+        x_rows = {}
+
+        def load_x(h):
             x_raw = slot("wide%d" % h, PACK * F, BF16)
-            x_rows.append(x_raw[:].rearrange("p (j w) -> p j w", j=PACK))
+            x_rows[h] = x_raw[:].rearrange("p (j w) -> p j w", j=PACK)
             load(x_rows[h], by_node(xg_gate[0, :, :], h))
 
-        def transpose_pairs(words, banks, order):
+        def transpose_pairs(words, banks, order, on_vector):
             grouped = grouped_tile()
             for b in range(2):
                 turned = bank(banks[b])
@@ -233,49 +216,56 @@ def tile_dgggl_pa_v_kernel(tc, xg_gate, gate_w_z, gate_b_z, xt, state1, state2, 
                 else:
                     dst = grouped[:].bitcast(F32).rearrange("q (j p u) -> q j p u", j=PACK, u=2)[:, 2 * b:2 * b + 2, :, :]
                     src = turned[:].rearrange("q (j u p) -> q j p u", j=2, u=2)
-                nc.scalar.copy(out=dst, in_=src)
+                copy(on_vector, dst, src)
             return grouped
 
         w_mx, dzf_mx, dzn_mx, x_mx = {}, {}, {}, {}
 
-        def turn_w(g):
-            staged["w", g] = transpose_pairs(w_words[g], (2 * (g % 2), 2 * (g % 2) + 1), "rows")
+        def turn_w(g, banks, on_vector=False):
+            staged["w", g] = transpose_pairs(w_words[g], banks, "rows", on_vector)
 
         def quant_w(g):
             w_mx[g] = quantize(staged["w", g], 12 + g, E4M3)
 
-        def turn_dz(h, banks):
+        def turn_dz(h, banks, on_vector=False):
             words = dz_sb[h][:].bitcast(F32).rearrange("p (j x) -> p j x", j=PACK)
-            staged["dzf", h] = transpose_pairs(words, banks, "tiles")
+            staged["dzf", h] = transpose_pairs(words, banks, "tiles", on_vector)
 
         def quant_dzf(h):
             dzf_mx[h] = quantize(staged["dzf", h], 8 + h, E5M2)
 
-        def copy_dzn(h):
-            staged["dzn", h] = interleave(True, dz_sb[h][:].rearrange("p (j w) -> p j w", j=PACK))
+        def copy_dzn(h, on_vector=True):
+            staged["dzn", h] = interleave(on_vector, dz_sb[h][:].rearrange("p (j w) -> p j w", j=PACK))
 
         def quant_dzn(h):
             dzn_mx[h] = quantize(staged["dzn", h], 10 + h, E5M2)
 
-        def copy_x(c, h):
-            staged["x", c, h] = interleave(True, x_rows[h][:, :, c * KP:(c + 1) * KP])
+        def copy_x(c, h, on_vector=True):
+            staged["x", c, h] = interleave(on_vector, x_rows[h][:, :, c * KP:(c + 1) * KP])
 
         def quant_x(c, h):
             index = 2 * c + h
             x_mx[c, h] = quantize(staged["x", c, h], index if index < 8 else index + 9, E4M3)
 
-        stage_order = (0, 1, 2, 3, 6, 7, 4, 5)
+        def out0_chunk(h, g, tag, banks):
+            result = slot(tag, UNIT, F32)
+            for t in range(PACK):
+                acc = bank(banks[t])
+                multiply(acc, dzf_mx[h], t, w_mx[g], True, True)
+                nc.scalar.copy(out=result[:, t * KP:(t + 1) * KP], in_=acc[:])
+            nc.sync.dma_start(out=by_node(out_0[0, :, g * KP:(g + 1) * KP], h),
+                              in_=result[:].rearrange("p (j w) -> p j w", j=PACK))
 
-        def out0_tile(h, t, banks):
-            result = slot("stage%d" % stage_order[PACK * h + t], F, F32)
+        def out0_tile(h, t, tag, banks, vector_chunks=()):
+            result = slot(tag, F, F32)
             for g in range(CHUNKS):
                 acc = bank(banks[(CHUNKS * t + g) % len(banks)])
                 multiply(acc, dzf_mx[h], t, w_mx[g], True, True)
-                nc.scalar.copy(out=result[:, g * KP:(g + 1) * KP], in_=acc[:])
+                copy(g in vector_chunks, result[:, g * KP:(g + 1) * KP], acc[:])
             nc.sync.dma_start(out=by_node(out_0[0, :, :], h)[:, t, :], in_=result[:])
 
-        def out1_chunk(c, vector_tiles):
-            result = slot("stage%d" % stage_order[c], UNIT, F32)
+        def out1_chunk(c, tag, vector_tiles):
+            result = slot(tag, UNIT, F32)
             for i in range(PACK):
                 acc = bank((PACK * c + i) % 8)
                 for h in range(HALVES):
@@ -284,48 +274,119 @@ def tile_dgggl_pa_v_kernel(tc, xg_gate, gate_w_z, gate_b_z, xt, state1, state2, 
             nc.sync.dma_start(out=out_1[c * KP:(c + 1) * KP, :].rearrange("(i p) n -> p i n", p=P),
                               in_=result[:].rearrange("p (i n) -> p i n", i=PACK))
 
-        add_product(0)
-        turn_w(0)
-        turn_w(1)
+        copy_g(0, True)
+        quant_g(0)
+        copy_a(0, 0, True)
+        copy_a(0, 1, False)
+        copy_g(1, True)
+        quant_a(0, 0)
+        dh_pass(0, 0)
+        quant_g(1)
+        quant_a(0, 1)
+        dh_pass(0, 1)
+        copy_a(1, 0, True)
+        copy_a(1, 1, False)
+        copy_g(2, False)
+        quant_a(1, 0)
+        dh_pass(1, 0)
+        quant_a(1, 1)
+        dh_pass(1, 1)
+        copy_a(2, 0, True)
+        quant_g(2)
+        copy_g(3, False)
+        quant_a(2, 0)
+        dh_pass(2, 0)
+        copy_a(3, 0, True)
+        copy_a(2, 1, False)
+        quant_g(3)
+        quant_a(3, 0)
+        dh_pass(3, 0)
+        copy_a(3, 1, True)
+        load_x(0)
+        load_x(1)
+        empty_dh(0, False)
         quant_a(2, 1)
-        round_dz(0)
-        dh_pass(2, 1)
         quant_a(3, 1)
-        turn_w(2)
-        quant_w(0)
-        turn_w(3)
-        quant_w(1)
-        turn_w(4)
-        turn_dz(0, (2, 3))
+        dh_pass(2, 1)
         dh_pass(3, 1)
-        quant_w(2)
-        quant_w(3)
-        quant_w(4)
-        quant_dzf(0)
-
-        for t in range(PACK):
-            out0_tile(0, t, (0, 1, 2, 3))
-
-        add_direct(1)
+        empty_dh(1, False)
+        gate_slope(0)
+        times_state(0)
+        add_product(0, 0, 0)
+        add_product(0, 1, 1)
+        add_direct(0, 0)
+        add_direct(0, 1)
+        add_product(0, 2, 2)
+        add_product(0, 3, 3)
+        add_direct(0, 2)
+        add_direct(0, 3)
+        round_dz(0, 0)
+        round_dz(0, 1)
+        round_dz(0, 2)
+        round_dz(0, 3)
+        turn_w(0, (4, 5))
+        add_product(1, 0, 0)
+        add_direct(1, 0)
+        add_product(1, 1, 1)
+        add_direct(1, 1)
+        quant_w(0)
+        turn_dz(0, (6, 7))
+        turn_w(1, (4, 5))
         gate_slope(1)
-        add_product(1)
+        quant_dzf(0)
+        out0_chunk(0, 0, "stage0", (2, 3, 6, 7))
+        quant_w(1)
+        turn_w(2, (4, 5))
         times_state(1)
-        round_dz(1)
-        turn_dz(1, (4, 5))
+        out0_chunk(0, 1, "stage1", (2, 3, 6, 7))
+        quant_w(2)
+        round_dz(1, 0)
+        round_dz(1, 1)
+        turn_w(3, (4, 5))
+        add_product(1, 2, 0)
+        add_direct(1, 2)
         copy_dzn(0)
-        quant_dzf(1)
-
-        for t in range(PACK):
-            out0_tile(1, t, (6, 7, 0, 1, 2, 3, 4, 5))
-
-        copy_dzn(1)
+        out0_chunk(0, 2, "stage2", (2, 3, 6, 7))
+        quant_w(3)
+        turn_w(4, (4, 5))
+        add_product(1, 3, 1)
+        add_direct(1, 3)
         quant_dzn(0)
+        round_dz(1, 2)
+        round_dz(1, 3)
+        out0_chunk(0, 3, "stage3", (2, 3, 6, 7))
+        quant_w(4)
+        turn_dz(1, (4, 5))
+        copy_dzn(1)
+        out0_chunk(0, 4, "stage6", (2, 3, 6, 7))
+        quant_dzf(1)
         copy_x(0, 0)
         quant_dzn(1)
-        for c in range(CHUNKS):
-            copy_x(c, 1)
-            quant_x(c, 0)
-            if c + 1 < CHUNKS:
-                copy_x(c + 1, 0)
-            quant_x(c, 1)
-            out1_chunk(c, (1, 3) if c == CHUNKS - 1 else ())
+        out0_tile(1, 0, "stage7", (2, 3, 6, 7, 4, 5, 0, 1))
+        out0_tile(1, 1, "stage4", (2, 3, 6, 7, 4, 5, 0, 1))
+        out0_tile(1, 2, "stage5", (2, 3, 6, 7, 4, 5, 0, 1))
+        out0_tile(1, 3, "stage0", (2, 3, 6, 7, 4, 5, 0, 1))
+        copy_x(0, 1)
+        quant_x(0, 0)
+        copy_x(1, 0)
+        quant_x(0, 1)
+        copy_x(1, 1)
+        quant_x(1, 0)
+        copy_x(2, 0)
+        quant_x(1, 1)
+        copy_x(2, 1)
+        quant_x(2, 0)
+        copy_x(3, 0)
+        quant_x(2, 1)
+        copy_x(3, 1)
+        quant_x(3, 0)
+        copy_x(4, 0)
+        quant_x(3, 1)
+        copy_x(4, 1)
+        quant_x(4, 0)
+        quant_x(4, 1)
+        out1_chunk(0, "stage1", ())
+        out1_chunk(1, "stage2", ())
+        out1_chunk(2, "stage3", ())
+        out1_chunk(3, "stage6", (1, 3))
+        out1_chunk(4, "stage7", (1, 3))

@@ -80,16 +80,20 @@ def tile_dgggl_pa_v_kernel(tc, xg_gate, gate_w_z, gate_b_z, xt, state1, state2, 
         def load(tile_ap, src):
             nc.sync.dma_start(out=tile_ap, in_=src)
 
-        g_raw = [slot("stage0", 2 * UNIT, BF16), slot("stage1", 2 * UNIT, BF16)]
+        g_raw = slot("big0", 4 * UNIT, BF16)
         a_raw = [slot("wide0", 4 * UNIT, BF16), slot("wide1", 4 * UNIT, BF16)]
         g_rows, a_rows = [], []
         for q in range(NS * HALVES):
             s, h = divmod(q, HALVES)
-            g_rows.append(g_raw[s][:].rearrange("p (h j w) -> p h j w", h=HALVES, j=PACK)[:, h, :, :])
+            g_rows.append(g_raw[:].rearrange("p (q j w) -> p q j w", q=NS * HALVES, j=PACK)[:, q, :, :])
             a_rows.append(a_raw[s][:].rearrange("p (h j w) -> p h j w", h=HALVES, j=PACK)[:, h, :, :])
 
         direct = grad_out[0, :, :].rearrange("n (s x) -> (n s) x", s=NS)
-        p_raw, z_sb, st_sb = {}, {}, {}
+        z_tiles = [slot("stage3", UNIT, F32), slot("stage5", UNIT, F32)]
+        p_tiles = [slot("stage2", 2 * UNIT, BF16), slot("stage4", 2 * UNIT, BF16)]
+        z_sb = [tile[:] for tile in z_tiles]
+        p_raw = [tile[:] for tile in p_tiles]
+        st_sb = slot("state", HALVES * UNIT, BF16)
 
         def load_g(q):
             s, h = divmod(q, HALVES)
@@ -101,16 +105,16 @@ def tile_dgggl_pa_v_kernel(tc, xg_gate, gate_w_z, gate_b_z, xt, state1, state2, 
             load(a_rows[q], by_node(supports[s, 0, :, :], h))
 
         def load_direct(h):
-            p_raw[h] = slot("stage%d" % (2 + 2 * h), 2 * UNIT, BF16)
-            load(p_raw[h][:].rearrange("p (r c) -> p r c", c=D),
+            load(p_raw[h].rearrange("p (r c) -> p r c", c=D),
                  direct[h * NS * KP:(h + 1) * NS * KP, DIN:DIN + D].rearrange("(p r) c -> p r c", r=PACK * NS))
 
-        def load_gate(h):
-            z_sb[h] = slot("stage%d" % (3 + 2 * h), UNIT, F32)
-            st_sb[h] = slot("state%d" % h, UNIT, BF16)
-            load(z_sb[h][:].rearrange("p (j w) -> p j w", j=PACK), by_node(z[0, :, :], h))
+        def load_z(h):
+            load(z_sb[h].rearrange("p (j w) -> p j w", j=PACK), by_node(z[0, :, :], h))
+
+        def load_states():
             for s, state in enumerate((state1, state2)):
-                load(st_sb[h][:].rearrange("p (s j c) -> p s j c", s=2, j=PACK)[:, s, :, :], by_node(state[0, :, :], h))
+                load(st_sb[:].rearrange("p (s h x) -> p s h x", s=2, h=HALVES)[:, s, :, :],
+                     state[0, :, :].rearrange("(h p j) c -> p h (j c)", h=HALVES, j=PACK))
 
         w_words = []
 
@@ -130,10 +134,11 @@ def tile_dgggl_pa_v_kernel(tc, xg_gate, gate_w_z, gate_b_z, xt, state1, state2, 
         load_g(3)
         load_a(3)
         load_direct(0)
-        load_gate(0)
+        load_z(0)
+        load_states()
         load_w("stage6", 0, 2)
         load_direct(1)
-        load_gate(1)
+        load_z(1)
         load_w("w_last", 2, 3)
 
         dh = {}
@@ -173,19 +178,19 @@ def tile_dgggl_pa_v_kernel(tc, xg_gate, gate_w_z, gate_b_z, xt, state1, state2, 
                                  rhs=ident[:], start=f == 0, stop=False, is_transpose=True)
 
         def add_direct(h, t):
-            terms = p_raw[h][:].rearrange("p (j s c) -> p j s c", j=PACK, s=NS)
+            terms = p_raw[h].rearrange("p (j s c) -> p j s c", j=PACK, s=NS)
             for s in range(NS):
                 nc.tensor.matmul(out=total[h, t][:], lhsT=ident_bf[:], rhs=terms[:, t, s, :], start=False,
                                  stop=s == NS - 1)
 
         def gate_slope(h):
-            nc.vector.scalar_tensor_tensor(out=z_sb[h][:], in0=z_sb[h][:], scalar=1.0, in1=z_sb[h][:],
+            nc.vector.scalar_tensor_tensor(out=z_sb[h], in0=z_sb[h], scalar=1.0, in1=z_sb[h],
                                            op0=ALU.subtract, op1=ALU.mult)
 
         def times_state(h):
-            factor = z_sb[h][:].rearrange("p (j s c) -> p j s c", j=PACK, s=2)
+            factor = z_sb[h].rearrange("p (j s c) -> p j s c", j=PACK, s=2)
             nc.vector.tensor_tensor(out=factor, in0=factor,
-                                    in1=st_sb[h][:].rearrange("p (s j c) -> p j s c", s=2, j=PACK), op=ALU.mult)
+                                    in1=st_sb[:].rearrange("p (s h j c) -> p h j s c", s=2, h=HALVES, j=PACK)[:, h, :, :, :], op=ALU.mult)
 
         def round_dz(h, t):
             if t == 0:
@@ -228,14 +233,14 @@ def tile_dgggl_pa_v_kernel(tc, xg_gate, gate_w_z, gate_b_z, xt, state1, state2, 
             w_mx[g] = quantize(staged["w", g], 12 + g, E4M3)
 
         def turn_dz(h, banks, on_vector=False):
-            words = dz_sb[h][:].bitcast(F32).rearrange("p (j x) -> p j x", j=PACK)
+            words = dz_sb[h].bitcast(F32).rearrange("p (j x) -> p j x", j=PACK)
             staged["dzf", h] = transpose_pairs(words, banks, "tiles", on_vector)
 
         def quant_dzf(h):
             dzf_mx[h] = quantize(staged["dzf", h], 8 + h, E5M2)
 
         def copy_dzn(h, on_vector=True):
-            staged["dzn", h] = interleave(on_vector, dz_sb[h][:].rearrange("p (j w) -> p j w", j=PACK))
+            staged["dzn", h] = interleave(on_vector, dz_sb[h].rearrange("p (j w) -> p j w", j=PACK))
 
         def quant_dzn(h):
             dzn_mx[h] = quantize(staged["dzn", h], 10 + h, E5M2)
@@ -247,14 +252,19 @@ def tile_dgggl_pa_v_kernel(tc, xg_gate, gate_w_z, gate_b_z, xt, state1, state2, 
             index = 2 * c + h
             x_mx[c, h] = quantize(staged["x", c, h], index if index < 8 else index + 9, E4M3)
 
+        gathered = {}
+
         def out0_chunk(h, g, tag, banks):
-            result = slot(tag, UNIT, F32)
+            first, count = (0, 2) if g < 2 else (g, 1)
+            if g == first:
+                result = slot(tag, count * UNIT, F32)
+                gathered[first] = result[:].rearrange("p (j w) -> p j w", j=PACK)
             for t in range(PACK):
                 acc = bank(banks[t])
                 multiply(acc, dzf_mx[h], t, w_mx[g], True, True)
-                nc.scalar.copy(out=result[:, t * KP:(t + 1) * KP], in_=acc[:])
-            nc.sync.dma_start(out=by_node(out_0[0, :, g * KP:(g + 1) * KP], h),
-                              in_=result[:].rearrange("p (j w) -> p j w", j=PACK))
+                nc.scalar.copy(out=gathered[first][:, t, (g - first) * KP:(g - first + 1) * KP], in_=acc[:])
+            if g == first + count - 1:
+                nc.sync.dma_start(out=by_node(out_0[0, :, first * KP:(first + count) * KP], h), in_=gathered[first])
 
         def out0_tile(h, t, tag, banks, vector_chunks=()):
             result = slot(tag, F, F32)
@@ -301,17 +311,15 @@ def tile_dgggl_pa_v_kernel(tc, xg_gate, gate_w_z, gate_b_z, xt, state1, state2, 
         quant_g(3)
         quant_a(3, 0)
         dh_pass(3, 0)
-        copy_a(3, 1, True)
+        empty_dh(0, False)
+        copy_a(3, 1, False)
         load_x(0)
         load_x(1)
-        empty_dh(0, False)
         quant_a(2, 1)
-        quant_a(3, 1)
         dh_pass(2, 1)
-        dh_pass(3, 1)
-        empty_dh(1, False)
         gate_slope(0)
         times_state(0)
+        quant_a(3, 1)
         add_product(0, 0, 0)
         add_product(0, 1, 1)
         add_direct(0, 0)
@@ -320,54 +328,56 @@ def tile_dgggl_pa_v_kernel(tc, xg_gate, gate_w_z, gate_b_z, xt, state1, state2, 
         add_product(0, 3, 3)
         add_direct(0, 2)
         add_direct(0, 3)
+        dh_pass(3, 1)
+        empty_dh(1, False)
         round_dz(0, 0)
         round_dz(0, 1)
         round_dz(0, 2)
         round_dz(0, 3)
         turn_w(0, (4, 5))
+        turn_dz(0, (6, 7))
         add_product(1, 0, 0)
         add_direct(1, 0)
+        quant_w(0)
+        turn_w(1, (4, 5))
+        quant_dzf(0)
+        gate_slope(1)
+        out0_chunk(0, 0, "big0", (2, 3, 6, 7))
+        quant_w(1)
+        times_state(1)
         add_product(1, 1, 1)
         add_direct(1, 1)
-        quant_w(0)
-        turn_dz(0, (6, 7))
-        turn_w(1, (4, 5))
-        gate_slope(1)
-        quant_dzf(0)
-        out0_chunk(0, 0, "stage0", (2, 3, 6, 7))
-        quant_w(1)
         turn_w(2, (4, 5))
-        times_state(1)
-        out0_chunk(0, 1, "stage1", (2, 3, 6, 7))
-        quant_w(2)
+        out0_chunk(0, 1, "big0", (2, 3, 6, 7))
         round_dz(1, 0)
         round_dz(1, 1)
-        turn_w(3, (4, 5))
+        quant_w(2)
         add_product(1, 2, 0)
         add_direct(1, 2)
+        turn_w(3, (4, 5))
         copy_dzn(0)
         out0_chunk(0, 2, "stage2", (2, 3, 6, 7))
+        round_dz(1, 2)
         quant_w(3)
-        turn_w(4, (4, 5))
         add_product(1, 3, 1)
         add_direct(1, 3)
+        turn_w(4, (4, 5))
         quant_dzn(0)
-        round_dz(1, 2)
+        copy_x(0, 0)
         round_dz(1, 3)
-        out0_chunk(0, 3, "stage3", (2, 3, 6, 7))
+        out0_chunk(0, 3, "stage7", (2, 3, 6, 7))
         quant_w(4)
         turn_dz(1, (4, 5))
         copy_dzn(1)
+        quant_x(0, 0)
         out0_chunk(0, 4, "stage6", (2, 3, 6, 7))
         quant_dzf(1)
-        copy_x(0, 0)
         quant_dzn(1)
-        out0_tile(1, 0, "stage7", (2, 3, 6, 7, 4, 5, 0, 1))
-        out0_tile(1, 1, "stage4", (2, 3, 6, 7, 4, 5, 0, 1))
-        out0_tile(1, 2, "stage5", (2, 3, 6, 7, 4, 5, 0, 1))
-        out0_tile(1, 3, "stage0", (2, 3, 6, 7, 4, 5, 0, 1))
+        out0_tile(1, 0, "stage4", (2, 3, 6, 7, 4, 5, 0, 1))
+        out0_tile(1, 1, "stage5", (2, 3, 6, 7, 4, 5, 0, 1))
+        out0_tile(1, 2, "big0", (2, 3, 6, 7, 4, 5, 0, 1))
+        out0_tile(1, 3, "stage3", (2, 3, 6, 7, 4, 5, 0, 1))
         copy_x(0, 1)
-        quant_x(0, 0)
         copy_x(1, 0)
         quant_x(0, 1)
         copy_x(1, 1)
@@ -385,8 +395,8 @@ def tile_dgggl_pa_v_kernel(tc, xg_gate, gate_w_z, gate_b_z, xt, state1, state2, 
         copy_x(4, 1)
         quant_x(4, 0)
         quant_x(4, 1)
-        out1_chunk(0, "stage1", ())
-        out1_chunk(1, "stage2", ())
-        out1_chunk(2, "stage3", ())
-        out1_chunk(3, "stage6", (1, 3))
-        out1_chunk(4, "stage7", (1, 3))
+        out1_chunk(0, "stage7", ())
+        out1_chunk(1, "stage6", ())
+        out1_chunk(2, "stage4", ())
+        out1_chunk(3, "stage5", (1, 3))
+        out1_chunk(4, "big0", (1, 3))

@@ -62,6 +62,12 @@ def tile_dgggl_pa_v_kernel(tc, xg_gate, gate_w_z, gate_b_z, xt, state1, state2, 
                  rows.rearrange("p j (c i) -> p c j i", i=PACK))
             return grouped
 
+        def interleave_sorted(on_vector, rows):
+            grouped = grouped_tile()
+            copy(on_vector, grouped[:].rearrange("p (t a b j) -> p a t b j", t=PACK, b=2, j=PACK),
+                 rows.rearrange("p j (a b t) -> p a t b j", b=2, t=PACK))
+            return grouped
+
         def quantize(grouped, index, fmt):
             codes = slot("codes%d" % index, KP, U32)
             scales = slot("scales%d" % index, KP, U8)
@@ -246,7 +252,7 @@ def tile_dgggl_pa_v_kernel(tc, xg_gate, gate_w_z, gate_b_z, xt, state1, state2, 
             dzn_mx[h] = quantize(staged["dzn", h], 10 + h, E5M2)
 
         def copy_x(c, h, on_vector=True):
-            staged["x", c, h] = interleave(on_vector, x_rows[h][:, :, c * KP:(c + 1) * KP])
+            staged["x", c, h] = interleave_sorted(on_vector, x_rows[h][:, :, c * KP:(c + 1) * KP])
 
         def quant_x(c, h):
             index = 2 * c + h
@@ -281,8 +287,7 @@ def tile_dgggl_pa_v_kernel(tc, xg_gate, gate_w_z, gate_b_z, xt, state1, state2, 
                 for h in range(HALVES):
                     multiply(acc, x_mx[c, h], i, dzn_mx[h], h == 0, h == HALVES - 1)
                 copy(i in vector_tiles, result[:, i * D:(i + 1) * D], acc[:])
-            nc.sync.dma_start(out=out_1[c * KP:(c + 1) * KP, :].rearrange("(i p) n -> p i n", p=P),
-                              in_=result[:].rearrange("p (i n) -> p i n", i=PACK))
+            nc.sync.dma_start(out=out_1[c * KP:(c + 1) * KP, :].rearrange("(p i) n -> p (i n)", i=PACK), in_=result[:])
 
         copy_g(0, True)
         quant_g(0)

@@ -4,13 +4,12 @@ import concourse.mybir as mybir
 from concourse.masks import make_identity
 
 N, F, D = 1024, 2560, 512
-DS = 256
 DIN = 128
-TERM = 640
+TERM = DIN + D
 NS = 2
 
 FLOPS = 2 * (NS * N * N * D + 2 * N * D * F)
-BYTES = 2 * (N * F + F * D + N * D + NS * N * N + 4 * N * D) + 4 * (N * D + N * F + F * D)
+BYTES = 2 * (N * F + F * D + N * D + NS * N * N + 2 * NS * N * D) + 4 * (N * D + N * F + F * D)
 
 F32 = mybir.dt.float32
 BF16 = mybir.dt.bfloat16
@@ -26,6 +25,12 @@ KP = P * PACK
 UNIT = KP * PACK
 HALVES = N // KP
 CHUNKS = F // KP
+PASSES = NS * HALVES
+BANKS = 8
+UNIT_BUFS = 6
+
+A_SLOT, G_SLOT, W_SLOT = 0, PASSES * HALVES, PASSES * HALVES + PASSES
+X_EXTRA_SLOT = W_SLOT + CHUNKS
 
 
 def tile_dgggl_pa_v_kernel(tc, xg_gate, gate_w_z, gate_b_z, xt, state1, state2, supports, z, grad_out,
@@ -53,25 +58,19 @@ def tile_dgggl_pa_v_kernel(tc, xg_gate, gate_w_z, gate_b_z, xt, state1, state2, 
             else:
                 nc.scalar.copy(out=out, in_=in_)
 
-        def grouped_tile():
-            return sb.tile([P, UNIT], BF16, name="grouped", tag="grouped", bufs=6, align_bytes=64)
+        def unit_tile():
+            return sb.tile([P, UNIT], BF16, name="unit", tag="unit", bufs=UNIT_BUFS, align_bytes=64)
 
         def interleave(on_vector, rows):
-            grouped = grouped_tile()
-            copy(on_vector, grouped[:].rearrange("p (c i j) -> p c j i", i=PACK, j=PACK),
+            unit = unit_tile()
+            copy(on_vector, unit[:].rearrange("p (c i j) -> p c j i", i=PACK, j=PACK),
                  rows.rearrange("p j (c i) -> p c j i", i=PACK))
-            return grouped
+            return unit
 
-        def interleave_sorted(on_vector, rows):
-            grouped = grouped_tile()
-            copy(on_vector, grouped[:].rearrange("p (t a b j) -> p a t b j", t=PACK, b=2, j=PACK),
-                 rows.rearrange("p j (a b t) -> p a t b j", b=2, t=PACK))
-            return grouped
-
-        def quantize(grouped, index, fmt):
+        def quantize(unit, index, fmt):
             codes = slot("codes%d" % index, KP, U32)
             scales = slot("scales%d" % index, KP, U8)
-            nc.vector.quantize_mx(out=codes[:].bitcast(fmt), scales=scales[:], in_=grouped[:])
+            nc.vector.quantize_mx(out=codes[:].bitcast(fmt), scales=scales[:], in_=unit[:])
             return codes, scales, fmt
 
         def multiply(acc, stationary, tile, moving, start, stop):
@@ -86,322 +85,272 @@ def tile_dgggl_pa_v_kernel(tc, xg_gate, gate_w_z, gate_b_z, xt, state1, state2, 
         def load(tile_ap, src):
             nc.sync.dma_start(out=tile_ap, in_=src)
 
-        g_raw = slot("big0", 4 * UNIT, BF16)
-        a_raw = [slot("wide0", 4 * UNIT, BF16), slot("wide1", 4 * UNIT, BF16)]
-        g_rows, a_rows = [], []
-        for q in range(NS * HALVES):
-            s, h = divmod(q, HALVES)
-            g_rows.append(g_raw[:].rearrange("p (q j w) -> p q j w", q=NS * HALVES, j=PACK)[:, q, :, :])
-            a_rows.append(a_raw[s][:].rearrange("p (h j w) -> p h j w", h=HALVES, j=PACK)[:, h, :, :])
+        grad_rows = grad_out[0, :, :].rearrange("n (s x) -> (n s) x", s=NS)
 
-        direct = grad_out[0, :, :].rearrange("n (s x) -> (n s) x", s=NS)
-        z_tiles = [slot("stage3", UNIT, F32), slot("stage5", UNIT, F32)]
-        p_tiles = [slot("stage2", 2 * UNIT, BF16), slot("stage4", 2 * UNIT, BF16)]
-        z_sb = [tile[:] for tile in z_tiles]
-        p_raw = [tile[:] for tile in p_tiles]
-        st_sb = slot("state", HALVES * UNIT, BF16)
+        def load_terms(tile_ap, h, first_col):
+            rows = grad_rows[h * NS * KP:(h + 1) * NS * KP, first_col:first_col + D]
+            load(tile_ap.rearrange("p (r c) -> p r c", c=D), rows.rearrange("(p r) c -> p r c", r=PACK * NS))
 
-        def load_g(q):
-            s, h = divmod(q, HALVES)
-            first = (2 * s + 1) * TERM + DIN
-            load(g_rows[q], by_node(grad_out[0, :, :][:, first:first + D], h))
+        g_raw = slot("big", PASSES * UNIT, BF16)
+        g_rows = g_raw[:].rearrange("p (h j s c) -> p h s j c", h=HALVES, j=PACK, s=NS)
+        a_rows = []
+        for h in range(HALVES):
+            load_terms(g_raw[:, h * NS * UNIT:(h + 1) * NS * UNIT], h, TERM + DIN)
+            a_raw = slot("wide%d" % h, NS * PACK * N, BF16)
+            a_rows.append(a_raw[:].rearrange("p (s j w) -> p s j w", s=NS, j=PACK))
+            for s in range(NS):
+                load(a_rows[h][:, s, :, :], by_node(supports[s, 0, :, :], h))
 
-        def load_a(q):
-            s, h = divmod(q, HALVES)
-            load(a_rows[q], by_node(supports[s, 0, :, :], h))
-
-        def load_direct(h):
-            load(p_raw[h].rearrange("p (r c) -> p r c", c=D),
-                 direct[h * NS * KP:(h + 1) * NS * KP, DIN:DIN + D].rearrange("(p r) c -> p r c", r=PACK * NS))
-
-        def load_z(h):
-            load(z_sb[h].rearrange("p (j w) -> p j w", j=PACK), by_node(z[0, :, :], h))
-
-        def load_states():
-            for s, state in enumerate((state1, state2)):
-                load(st_sb[:].rearrange("p (s h x) -> p s h x", s=2, h=HALVES)[:, s, :, :],
-                     state[0, :, :].rearrange("(h p j) c -> p h (j c)", h=HALVES, j=PACK))
-
+        p_raw = [slot("stage0", NS * UNIT, BF16), slot("stage1", NS * UNIT, BF16)]
+        gate = [slot("stage2", UNIT, F32), slot("stage3", UNIT, F32)]
+        states = slot("states", HALVES * UNIT, BF16)
         w_words = []
 
         def load_w(tag, first, count):
             w_raw = slot(tag, count * UNIT, BF16)
             load(w_raw[:].rearrange("p (g x) -> p g x", g=count),
                  gate_w_z[first * KP:(first + count) * KP, :].rearrange("(g p j) k -> p g (j k)", p=P, j=PACK))
-            for g in range(count):
-                w_words.append(w_raw[:].bitcast(F32).rearrange("p (g j x) -> p g j x", g=count, j=PACK)[:, g, :, :])
+            words = w_raw[:].bitcast(F32).rearrange("p (g j x) -> p g j x", g=count, j=PACK)
+            w_words.extend([words[:, g, :, :] for g in range(count)])
 
-        load_g(0)
-        load_a(0)
-        load_g(1)
-        load_a(1)
-        load_g(2)
-        load_a(2)
-        load_g(3)
-        load_a(3)
-        load_direct(0)
-        load_z(0)
-        load_states()
-        load_w("stage6", 0, 2)
-        load_direct(1)
-        load_z(1)
-        load_w("w_last", 2, 3)
+        load_terms(p_raw[0][:], 0, DIN)
+        load(gate[0][:].rearrange("p (j w) -> p j w", j=PACK), by_node(z[0, :, :], 0))
+        for i, state in enumerate((state1, state2)):
+            load(states[:].rearrange("p (i h x) -> p i h x", i=2, h=HALVES)[:, i, :, :],
+                 state[0, :, :].rearrange("(h p j) c -> p h (j c)", h=HALVES, j=PACK))
+        load_w("stage4", 0, 2)
+        load_terms(p_raw[1][:], 1, DIN)
+        load(gate[1][:].rearrange("p (j w) -> p j w", j=PACK), by_node(z[0, :, :], 1))
+        load_w("weight", 2, CHUNKS - 2)
 
-        dh = {}
-        g_mx, a_mx, staged = {}, {}, {}
+        units, g_mx, a_mx = {}, {}, {}
+        product = [[bank(PACK * m + f) for f in range(PACK)] for m in range(HALVES)]
 
         def copy_g(q, on_vector):
-            staged["g", q] = interleave(on_vector, g_rows[q])
-
-        def copy_a(q, h, on_vector):
-            staged["a", q, h] = interleave(on_vector, a_rows[q][:, :, h * KP:(h + 1) * KP])
+            h, s = divmod(q, NS)
+            units["g", q] = interleave(on_vector, g_rows[:, h, s, :, :])
 
         def quant_g(q):
-            g_mx[q] = quantize(staged["g", q], 8 + q, E5M2)
+            g_mx[q] = quantize(units["g", q], G_SLOT + q, E5M2)
 
-        def quant_a(q, h):
-            a_mx[q, h] = quantize(staged["a", q, h], 2 * q + h, E4M3)
+        def copy_a(q, m):
+            h, s = divmod(q, NS)
+            units["a", q, m] = interleave(m == 0, a_rows[h][:, s, :, m * KP:(m + 1) * KP])
 
-        def dh_pass(q, h):
-            if q == 0:
-                dh[h] = [bank(PACK * h + t) for t in range(PACK)]
-            for t in range(PACK):
-                multiply(dh[h][t], g_mx[q], t, a_mx[q, h], q == 0, q == NS * HALVES - 1)
+        def quant_a(q, m):
+            a_mx[q, m] = quantize(units["a", q, m], A_SLOT + HALVES * q + m, E4M3)
 
-        d_sb, total, dz_sb = {}, {}, {}
-
-        def empty_dh(h, on_vector):
-            d_sb[h] = slot("d%d" % h, UNIT, F32)
+        def product_pass(q, m):
             for f in range(PACK):
-                copy(on_vector, d_sb[h][:, f * KP:(f + 1) * KP].rearrange("q (t p) -> q t p", t=PACK),
-                     dh[h][f][:].rearrange("q (p t) -> q t p", t=PACK))
+                multiply(product[m][f], g_mx[q], f, a_mx[q, m], q == 0, q == PASSES - 1)
 
-        def add_product(h, t, b):
-            total[h, t] = bank(b)
+        for q in range(PASSES):
+            if q % NS == 0:
+                copy_g(q, True)
+                copy_g(q + 1, False)
+            copy_a(q, 0)
+            copy_a(q, 1)
+            quant_g(q)
+            quant_a(q, 0)
+            product_pass(q, 0)
+            if q > 0:
+                quant_a(q - 1, 1)
+                product_pass(q - 1, 1)
+        quant_a(PASSES - 1, 1)
+        product_pass(PASSES - 1, 1)
+
+        x_rows = []
+        for h in range(HALVES):
+            x_raw = slot("wide%d" % h, PACK * F, BF16)
+            x_rows.append(x_raw[:].rearrange("p (j w) -> p j w", j=PACK))
+            load(x_rows[h], by_node(xg_gate[0, :, :], h))
+
+        product_sb, dh, dz = [], {}, []
+
+        def empty_product(m):
+            sorted_nodes = slot("product%d" % m, UNIT, F32)
             for f in range(PACK):
-                first = f * KP + t * P
-                nc.tensor.matmul(out=total[h, t][:, f * P:(f + 1) * P], lhsT=d_sb[h][:, first:first + P],
+                nc.scalar.copy(out=sorted_nodes[:, f * KP:(f + 1) * KP].rearrange("q (j p) -> q j p", j=PACK),
+                               in_=product[m][f][:].rearrange("q (p j) -> q j p", j=PACK))
+            product_sb.append(sorted_nodes)
+
+        def turn_product(h, j, b):
+            dh[h, j] = bank(b)
+            for f in range(PACK):
+                first = f * KP + j * P
+                nc.tensor.matmul(out=dh[h, j][:, f * P:(f + 1) * P], lhsT=product_sb[h][:, first:first + P],
                                  rhs=ident[:], start=f == 0, stop=False, is_transpose=True)
 
-        def add_direct(h, t):
-            terms = p_raw[h].rearrange("p (j s c) -> p j s c", j=PACK, s=NS)
+        def add_direct(h, j):
+            terms = p_raw[h][:].rearrange("p (j s c) -> p j s c", j=PACK, s=NS)
             for s in range(NS):
-                nc.tensor.matmul(out=total[h, t][:], lhsT=ident_bf[:], rhs=terms[:, t, s, :], start=False,
+                nc.tensor.matmul(out=dh[h, j][:], lhsT=ident_bf[:], rhs=terms[:, j, s, :], start=False,
                                  stop=s == NS - 1)
 
         def gate_slope(h):
-            nc.vector.scalar_tensor_tensor(out=z_sb[h], in0=z_sb[h], scalar=1.0, in1=z_sb[h],
+            nc.vector.scalar_tensor_tensor(out=gate[h][:], in0=gate[h][:], scalar=1.0, in1=gate[h][:],
                                            op0=ALU.subtract, op1=ALU.mult)
 
         def times_state(h):
-            factor = z_sb[h].rearrange("p (j s c) -> p j s c", j=PACK, s=2)
-            nc.vector.tensor_tensor(out=factor, in0=factor,
-                                    in1=st_sb[:].rearrange("p (s h j c) -> p h j s c", s=2, h=HALVES, j=PACK)[:, h, :, :, :], op=ALU.mult)
+            factor = gate[h][:].rearrange("p (j i c) -> p j i c", j=PACK, i=2)
+            st = states[:].rearrange("p (i h j c) -> p h j i c", i=2, h=HALVES, j=PACK)[:, h, :, :, :]
+            nc.vector.tensor_tensor(out=factor, in0=factor, in1=st, op=ALU.mult)
 
-        def round_dz(h, t):
-            if t == 0:
-                dz_sb[h] = slot("dz%d" % h, UNIT, BF16)
-            cols = slice(t * D, (t + 1) * D)
-            nc.vector.scalar_tensor_tensor(out=dz_sb[h][:, cols], in0=total[h, t][:], scalar=-1.0,
-                                           in1=z_sb[h][:, cols], op0=ALU.mult, op1=ALU.mult)
+        def round_dz(h, j):
+            if j == 0:
+                dz.append(slot("dz%d" % h, UNIT, BF16))
+            cols = slice(j * D, (j + 1) * D)
+            nc.vector.scalar_tensor_tensor(out=dz[h][:, cols], in0=dh[h, j][:], scalar=-1.0, in1=gate[h][:, cols],
+                                           op0=ALU.mult, op1=ALU.mult)
 
-
-        x_rows = {}
-
-        def load_x(h):
-            x_raw = slot("wide%d" % h, PACK * F, BF16)
-            x_rows[h] = x_raw[:].rearrange("p (j w) -> p j w", j=PACK)
-            load(x_rows[h], by_node(xg_gate[0, :, :], h))
-
-        def transpose_pairs(words, banks, order, on_vector):
-            grouped = grouped_tile()
+        def transpose_unit(words, banks, columns):
+            unit = unit_tile()
+            dst = unit[:].bitcast(F32).rearrange("q (%s u) -> q j p u" % columns, j=PACK, u=2)
             for b in range(2):
                 turned = bank(banks[b])
                 for r in range(2):
                     for u in range(2):
                         k = 2 * r + u
                         nc.tensor.transpose(turned[:, k * P:(k + 1) * P], words[:, 2 * b + r, u:2 * P:2], ident[:])
-                if order == "rows":
-                    dst = grouped[:].bitcast(F32).rearrange("q (p j u) -> q p j u", j=PACK, u=2)[:, :, 2 * b:2 * b + 2, :]
-                    src = turned[:].rearrange("q (j u p) -> q p j u", j=2, u=2)
-                else:
-                    dst = grouped[:].bitcast(F32).rearrange("q (j p u) -> q j p u", j=PACK, u=2)[:, 2 * b:2 * b + 2, :, :]
-                    src = turned[:].rearrange("q (j u p) -> q j p u", j=2, u=2)
-                copy(on_vector, dst, src)
-            return grouped
+                walk = "q j p u -> q %s u" % columns
+                nc.scalar.copy(out=dst[:, 2 * b:2 * b + 2, :, :].rearrange(walk),
+                               in_=turned[:].rearrange("q (j u p) -> q j p u", j=2, u=2).rearrange(walk))
+            return unit
 
         w_mx, dzf_mx, dzn_mx, x_mx = {}, {}, {}, {}
 
-        def turn_w(g, banks, on_vector=False):
-            staged["w", g] = transpose_pairs(w_words[g], banks, "rows", on_vector)
+        def turn_w(g, banks):
+            units["w", g] = transpose_unit(w_words[g], banks, "p j")
 
         def quant_w(g):
-            w_mx[g] = quantize(staged["w", g], 12 + g, E4M3)
+            w_mx[g] = quantize(units["w", g], W_SLOT + g, E4M3)
 
-        def turn_dz(h, banks, on_vector=False):
-            words = dz_sb[h].bitcast(F32).rearrange("p (j x) -> p j x", j=PACK)
-            staged["dzf", h] = transpose_pairs(words, banks, "tiles", on_vector)
+        def turn_dz(h, banks):
+            units["dzf", h] = transpose_unit(dz[h][:].bitcast(F32).rearrange("p (j x) -> p j x", j=PACK), banks, "j p")
 
         def quant_dzf(h):
-            dzf_mx[h] = quantize(staged["dzf", h], 8 + h, E5M2)
+            dzf_mx[h] = quantize(units["dzf", h], G_SLOT + h, E5M2)
 
-        def copy_dzn(h, on_vector=True):
-            staged["dzn", h] = interleave(on_vector, dz_sb[h].rearrange("p (j w) -> p j w", j=PACK))
+        def copy_dzn(h):
+            units["dzn", h] = interleave(True, dz[h][:].rearrange("p (j w) -> p j w", j=PACK))
 
         def quant_dzn(h):
-            dzn_mx[h] = quantize(staged["dzn", h], 10 + h, E5M2)
+            dzn_mx[h] = quantize(units["dzn", h], G_SLOT + HALVES + h, E5M2)
 
-        def copy_x(c, h, on_vector=True):
-            staged["x", c, h] = interleave_sorted(on_vector, x_rows[h][:, :, c * KP:(c + 1) * KP])
+        def copy_x(c, h):
+            units["x", c, h] = interleave(True, x_rows[h][:, :, c * KP:(c + 1) * KP])
 
         def quant_x(c, h):
-            index = 2 * c + h
-            x_mx[c, h] = quantize(staged["x", c, h], index if index < 8 else index + 9, E4M3)
+            index = HALVES * c + h
+            x_mx[c, h] = quantize(units["x", c, h], A_SLOT + index if index < G_SLOT else X_EXTRA_SLOT + h, E4M3)
 
-        gathered = {}
+        def out0_chunk(g, result, banks):
+            for j in range(PACK):
+                acc = bank(banks[j])
+                multiply(acc, dzf_mx[0], j, w_mx[g], True, True)
+                nc.scalar.copy(out=result[:, j, :], in_=acc[:])
 
-        def out0_chunk(h, g, tag, banks):
-            first, count = (0, 2) if g < 2 else (g, 1)
-            if g == first:
-                result = slot(tag, count * UNIT, F32)
-                gathered[first] = result[:].rearrange("p (j w) -> p j w", j=PACK)
-            for t in range(PACK):
-                acc = bank(banks[t])
-                multiply(acc, dzf_mx[h], t, w_mx[g], True, True)
-                nc.scalar.copy(out=gathered[first][:, t, (g - first) * KP:(g - first + 1) * KP], in_=acc[:])
-            if g == first + count - 1:
-                nc.sync.dma_start(out=by_node(out_0[0, :, first * KP:(first + count) * KP], h), in_=gathered[first])
+        def result_rows(tag, chunks):
+            tile = slot(tag, chunks * UNIT, F32)
+            return tile[:].rearrange("p (j w) -> p j w", j=PACK)
 
-        def out0_tile(h, t, tag, banks, vector_chunks=()):
+        def store_out0_chunks(first, result):
+            nc.sync.dma_start(out=by_node(out_0[0, :, first * KP:first * KP + result.shape[2]], 0), in_=result)
+
+        def out0_tile(j, tag, banks):
             result = slot(tag, F, F32)
             for g in range(CHUNKS):
-                acc = bank(banks[(CHUNKS * t + g) % len(banks)])
-                multiply(acc, dzf_mx[h], t, w_mx[g], True, True)
-                copy(g in vector_chunks, result[:, g * KP:(g + 1) * KP], acc[:])
-            nc.sync.dma_start(out=by_node(out_0[0, :, :], h)[:, t, :], in_=result[:])
+                acc = bank(banks[(CHUNKS * j + g) % BANKS])
+                multiply(acc, dzf_mx[1], j, w_mx[g], True, True)
+                nc.scalar.copy(out=result[:, g * KP:(g + 1) * KP], in_=acc[:])
+            nc.sync.dma_start(out=by_node(out_0[0, :, :], 1)[:, j, :], in_=result[:])
 
-        def out1_chunk(c, tag, vector_tiles):
+        def out1_chunk(c, tag, shared):
             result = slot(tag, UNIT, F32)
             for i in range(PACK):
-                acc = bank((PACK * c + i) % 8)
+                acc = bank((PACK * c + i) % BANKS)
                 for h in range(HALVES):
                     multiply(acc, x_mx[c, h], i, dzn_mx[h], h == 0, h == HALVES - 1)
-                copy(i in vector_tiles, result[:, i * D:(i + 1) * D], acc[:])
-            nc.sync.dma_start(out=out_1[c * KP:(c + 1) * KP, :].rearrange("(p i) n -> p (i n)", i=PACK), in_=result[:])
+                copy(shared and i % 2 == 1, result[:, i * D:(i + 1) * D], acc[:])
+            nc.sync.dma_start(out=out_1[c * KP:(c + 1) * KP, :].rearrange("(i p) n -> p i n", p=P),
+                              in_=result[:].rearrange("p (i n) -> p i n", i=PACK))
 
-        copy_g(0, True)
-        quant_g(0)
-        copy_a(0, 0, True)
-        copy_a(0, 1, False)
-        copy_g(1, True)
-        quant_a(0, 0)
-        dh_pass(0, 0)
-        quant_g(1)
-        quant_a(0, 1)
-        dh_pass(0, 1)
-        copy_a(1, 0, True)
-        copy_a(1, 1, False)
-        copy_g(2, False)
-        quant_a(1, 0)
-        dh_pass(1, 0)
-        quant_a(1, 1)
-        dh_pass(1, 1)
-        copy_a(2, 0, True)
-        quant_g(2)
-        copy_g(3, False)
-        quant_a(2, 0)
-        dh_pass(2, 0)
-        copy_a(3, 0, True)
-        copy_a(2, 1, False)
-        quant_g(3)
-        quant_a(3, 0)
-        dh_pass(3, 0)
-        empty_dh(0, False)
-        copy_a(3, 1, False)
-        load_x(0)
-        load_x(1)
-        quant_a(2, 1)
-        dh_pass(2, 1)
+        empty_product(0)
+        empty_product(1)
         gate_slope(0)
         times_state(0)
-        quant_a(3, 1)
-        add_product(0, 0, 0)
-        add_product(0, 1, 1)
-        add_direct(0, 0)
-        add_direct(0, 1)
-        add_product(0, 2, 2)
-        add_product(0, 3, 3)
-        add_direct(0, 2)
-        add_direct(0, 3)
-        dh_pass(3, 1)
-        empty_dh(1, False)
-        round_dz(0, 0)
-        round_dz(0, 1)
-        round_dz(0, 2)
-        round_dz(0, 3)
-        turn_w(0, (4, 5))
-        turn_dz(0, (6, 7))
-        add_product(1, 0, 0)
-        add_direct(1, 0)
+        for j0 in (0, 2):
+            for j in (j0, j0 + 1):
+                turn_product(0, j, j)
+            for j in (j0, j0 + 1):
+                add_direct(0, j)
+        for j in range(PACK):
+            round_dz(0, j)
+
+        w_banks, out_banks = (4, 5), (2, 3, 6, 7)
+
+        def sum_dh(j):
+            turn_product(1, j, j % 2)
+            add_direct(1, j)
+
+        turn_w(0, w_banks)
+        sum_dh(0)
         quant_w(0)
-        turn_w(1, (4, 5))
+        turn_dz(0, (6, 7))
+        turn_w(1, w_banks)
         quant_dzf(0)
         gate_slope(1)
-        out0_chunk(0, 0, "big0", (2, 3, 6, 7))
+
+        pair = result_rows("big", 2)
+        out0_chunk(0, pair[:, :, :KP], out_banks)
         quant_w(1)
         times_state(1)
-        add_product(1, 1, 1)
-        add_direct(1, 1)
-        turn_w(2, (4, 5))
-        out0_chunk(0, 1, "big0", (2, 3, 6, 7))
+        sum_dh(1)
+        turn_w(2, w_banks)
+
+        out0_chunk(1, pair[:, :, KP:], out_banks)
+        store_out0_chunks(0, pair)
         round_dz(1, 0)
         round_dz(1, 1)
         quant_w(2)
-        add_product(1, 2, 0)
-        add_direct(1, 2)
-        turn_w(3, (4, 5))
+        sum_dh(2)
+        turn_w(3, w_banks)
         copy_dzn(0)
-        out0_chunk(0, 2, "stage2", (2, 3, 6, 7))
+
+        single = result_rows("stage0", 1)
+        out0_chunk(2, single, out_banks)
+        store_out0_chunks(2, single)
         round_dz(1, 2)
         quant_w(3)
-        add_product(1, 3, 1)
-        add_direct(1, 3)
-        turn_w(4, (4, 5))
+        sum_dh(3)
+        turn_w(4, w_banks)
         quant_dzn(0)
         copy_x(0, 0)
         round_dz(1, 3)
-        out0_chunk(0, 3, "stage7", (2, 3, 6, 7))
+
+        single = result_rows("stage2", 1)
+        out0_chunk(3, single, out_banks)
+        store_out0_chunks(3, single)
         quant_w(4)
-        turn_dz(1, (4, 5))
+        turn_dz(1, w_banks)
         copy_dzn(1)
         quant_x(0, 0)
-        out0_chunk(0, 4, "stage6", (2, 3, 6, 7))
+
+        single = result_rows("stage4", 1)
+        out0_chunk(4, single, out_banks)
+        store_out0_chunks(4, single)
         quant_dzf(1)
         quant_dzn(1)
-        out0_tile(1, 0, "stage4", (2, 3, 6, 7, 4, 5, 0, 1))
-        out0_tile(1, 1, "stage5", (2, 3, 6, 7, 4, 5, 0, 1))
-        out0_tile(1, 2, "big0", (2, 3, 6, 7, 4, 5, 0, 1))
-        out0_tile(1, 3, "stage3", (2, 3, 6, 7, 4, 5, 0, 1))
-        copy_x(0, 1)
-        copy_x(1, 0)
-        quant_x(0, 1)
-        copy_x(1, 1)
-        quant_x(1, 0)
-        copy_x(2, 0)
-        quant_x(1, 1)
-        copy_x(2, 1)
-        quant_x(2, 0)
-        copy_x(3, 0)
-        quant_x(2, 1)
-        copy_x(3, 1)
-        quant_x(3, 0)
-        copy_x(4, 0)
-        quant_x(3, 1)
-        copy_x(4, 1)
-        quant_x(4, 0)
-        quant_x(4, 1)
-        out1_chunk(0, "stage7", ())
-        out1_chunk(1, "stage6", ())
-        out1_chunk(2, "stage4", ())
-        out1_chunk(3, "stage5", (1, 3))
-        out1_chunk(4, "big0", (1, 3))
+
+        for j, tag in enumerate(("stage1", "stage3", "weight", "big")):
+            out0_tile(j, tag, out_banks + w_banks + (0, 1))
+
+        order = [(c, h) for c in range(CHUNKS) for h in range(HALVES)]
+        copy_x(*order[1])
+        for i in range(1, len(order)):
+            if i + 1 < len(order):
+                copy_x(*order[i + 1])
+            quant_x(*order[i])
+
+        for c, tag in enumerate(("stage0", "stage2", "stage4", "stage1", "stage3")):
+            out1_chunk(c, tag, c >= CHUNKS - 2)

from contextlib import ExitStack

import concourse.mybir as mybir
from concourse.masks import make_identity

N, F, D = 1024, 2560, 512
DIN = 128
TERM = DIN + D
NS = 2

FLOPS = 2 * (NS * N * N * D + 2 * N * D * F)
BYTES = 2 * (N * F + F * D + N * D + NS * N * N + 2 * NS * N * D) + 4 * (N * D + N * F + F * D)

F32 = mybir.dt.float32
BF16 = mybir.dt.bfloat16
U32 = mybir.dt.uint32
U8 = mybir.dt.uint8
E4M3 = mybir.dt.float8_e4m3fn_x4
E5M2 = mybir.dt.float8_e5m2_x4
ALU = mybir.AluOpType

P = 128
PACK = 4
KP = P * PACK
UNIT = KP * PACK
HALVES = N // KP
CHUNKS = F // KP
PASSES = NS * HALVES
BANKS = 8
UNIT_BUFS = 6

A_SLOT, G_SLOT, W_SLOT = 0, PASSES * HALVES, PASSES * HALVES + PASSES
X_EXTRA_SLOT = W_SLOT + CHUNKS


def tile_dgggl_pa_v_kernel(tc, xg_gate, gate_w_z, gate_b_z, xt, state1, state2, supports, z, grad_out,
                                        out_0, out_1):
    nc = tc.nc
    with ExitStack() as ctx:
        sb = ctx.enter_context(tc.tile_pool(name="sb", bufs=1))
        ps = ctx.enter_context(tc.psum_pool(name="ps", bufs=1))

        ident = sb.tile([P, P], F32, name="ident")
        make_identity(nc, ident[:])
        ident_bf = sb.tile([P, P], BF16, name="ident_bf")
        make_identity(nc, ident_bf[:])
        ctx.enter_context(tc.manual_schedule())

        def slot(tag, width, dtype):
            return sb.tile([P, width], dtype, name=tag, tag=tag, align_bytes=64)

        def bank(b):
            return ps.tile([P, KP], F32, name="bank%d" % b, tag="bank%d" % b)

        def copy(on_vector, out, in_):
            if on_vector:
                nc.vector.tensor_copy(out=out, in_=in_)
            else:
                nc.scalar.copy(out=out, in_=in_)

        def unit_tile():
            return sb.tile([P, UNIT], BF16, name="unit", tag="unit", bufs=UNIT_BUFS, align_bytes=64)

        def interleave(on_vector, rows):
            unit = unit_tile()
            copy(on_vector, unit[:].rearrange("p (c i j) -> p c j i", i=PACK, j=PACK),
                 rows.rearrange("p j (c i) -> p c j i", i=PACK))
            return unit

        def quantize(unit, index, fmt):
            codes = slot("codes%d" % index, KP, U32)
            scales = slot("scales%d" % index, KP, U8)
            nc.vector.quantize_mx(out=codes[:].bitcast(fmt), scales=scales[:], in_=unit[:])
            return codes, scales, fmt

        def multiply(acc, stationary, tile, moving, start, stop):
            cols = slice(tile * P, (tile + 1) * P)
            nc.tensor.matmul_mx(out=acc[:], lhsT=stationary[0][:, cols].bitcast(stationary[2]),
                                lhsT_scale=stationary[1][:, cols], rhs=moving[0][:].bitcast(moving[2]),
                                rhs_scale=moving[1][:], start=start, stop=stop)

        def by_node(ap, h):
            return ap[h * KP:(h + 1) * KP, :].rearrange("(p j) w -> p j w", j=PACK)

        def load(tile_ap, src):
            nc.sync.dma_start(out=tile_ap, in_=src)

        grad_rows = grad_out[0, :, :].rearrange("n (s x) -> (n s) x", s=NS)

        def load_terms(tile_ap, h, first_col):
            rows = grad_rows[h * NS * KP:(h + 1) * NS * KP, first_col:first_col + D]
            load(tile_ap.rearrange("p (r c) -> p r c", c=D), rows.rearrange("(p r) c -> p r c", r=PACK * NS))

        g_raw = slot("big", PASSES * UNIT, BF16)
        g_rows = g_raw[:].rearrange("p (h j s c) -> p h s j c", h=HALVES, j=PACK, s=NS)
        a_rows = []
        for h in range(HALVES):
            load_terms(g_raw[:, h * NS * UNIT:(h + 1) * NS * UNIT], h, TERM + DIN)
            a_raw = slot("wide%d" % h, NS * PACK * N, BF16)
            a_rows.append(a_raw[:].rearrange("p (s j w) -> p s j w", s=NS, j=PACK))
            for s in range(NS):
                load(a_rows[h][:, s, :, :], by_node(supports[s, 0, :, :], h))

        p_raw = [slot("stage0", NS * UNIT, BF16), slot("stage1", NS * UNIT, BF16)]
        gate = [slot("stage2", UNIT, F32), slot("stage3", UNIT, F32)]
        states = slot("states", HALVES * UNIT, BF16)
        w_words = []

        def load_w(tag, first, count):
            w_raw = slot(tag, count * UNIT, BF16)
            load(w_raw[:].rearrange("p (g x) -> p g x", g=count),
                 gate_w_z[first * KP:(first + count) * KP, :].rearrange("(g p j) k -> p g (j k)", p=P, j=PACK))
            words = w_raw[:].bitcast(F32).rearrange("p (g j x) -> p g j x", g=count, j=PACK)
            w_words.extend([words[:, g, :, :] for g in range(count)])

        load_terms(p_raw[0][:], 0, DIN)
        load(gate[0][:].rearrange("p (j w) -> p j w", j=PACK), by_node(z[0, :, :], 0))
        for i, state in enumerate((state1, state2)):
            load(states[:].rearrange("p (i h x) -> p i h x", i=2, h=HALVES)[:, i, :, :],
                 state[0, :, :].rearrange("(h p j) c -> p h (j c)", h=HALVES, j=PACK))
        load_w("stage4", 0, 2)
        load_terms(p_raw[1][:], 1, DIN)
        load(gate[1][:].rearrange("p (j w) -> p j w", j=PACK), by_node(z[0, :, :], 1))
        load_w("weight", 2, CHUNKS - 2)

        units, g_mx, a_mx = {}, {}, {}
        product = [[bank(PACK * m + f) for f in range(PACK)] for m in range(HALVES)]

        def copy_g(q, on_vector):
            h, s = divmod(q, NS)
            units["g", q] = interleave(on_vector, g_rows[:, h, s, :, :])

        def quant_g(q):
            g_mx[q] = quantize(units["g", q], G_SLOT + q, E5M2)

        def copy_a(q, m):
            h, s = divmod(q, NS)
            units["a", q, m] = interleave(m == 0, a_rows[h][:, s, :, m * KP:(m + 1) * KP])

        def quant_a(q, m):
            a_mx[q, m] = quantize(units["a", q, m], A_SLOT + HALVES * q + m, E4M3)

        def product_pass(q, m):
            for f in range(PACK):
                multiply(product[m][f], g_mx[q], f, a_mx[q, m], q == 0, q == PASSES - 1)

        for q in range(PASSES):
            if q % NS == 0:
                copy_g(q, True)
                copy_g(q + 1, False)
            copy_a(q, 0)
            copy_a(q, 1)
            quant_g(q)
            quant_a(q, 0)
            product_pass(q, 0)
            if q > 0:
                quant_a(q - 1, 1)
                product_pass(q - 1, 1)
        quant_a(PASSES - 1, 1)
        product_pass(PASSES - 1, 1)

        x_rows = []
        for h in range(HALVES):
            x_raw = slot("wide%d" % h, PACK * F, BF16)
            x_rows.append(x_raw[:].rearrange("p (j w) -> p j w", j=PACK))
            load(x_rows[h], by_node(xg_gate[0, :, :], h))

        product_sb, dh, dz = [], {}, []

        def empty_product(m):
            sorted_nodes = slot("product%d" % m, UNIT, F32)
            for f in range(PACK):
                nc.scalar.copy(out=sorted_nodes[:, f * KP:(f + 1) * KP].rearrange("q (j p) -> q j p", j=PACK),
                               in_=product[m][f][:].rearrange("q (p j) -> q j p", j=PACK))
            product_sb.append(sorted_nodes)

        def turn_product(h, j, b):
            dh[h, j] = bank(b)
            for f in range(PACK):
                first = f * KP + j * P
                nc.tensor.matmul(out=dh[h, j][:, f * P:(f + 1) * P], lhsT=product_sb[h][:, first:first + P],
                                 rhs=ident[:], start=f == 0, stop=False, is_transpose=True)

        def add_direct(h, j):
            terms = p_raw[h][:].rearrange("p (j s c) -> p j s c", j=PACK, s=NS)
            for s in range(NS):
                nc.tensor.matmul(out=dh[h, j][:], lhsT=ident_bf[:], rhs=terms[:, j, s, :], start=False,
                                 stop=s == NS - 1)

        def gate_slope(h):
            nc.vector.scalar_tensor_tensor(out=gate[h][:], in0=gate[h][:], scalar=1.0, in1=gate[h][:],
                                           op0=ALU.subtract, op1=ALU.mult)

        def times_state(h):
            factor = gate[h][:].rearrange("p (j i c) -> p j i c", j=PACK, i=2)
            st = states[:].rearrange("p (i h j c) -> p h j i c", i=2, h=HALVES, j=PACK)[:, h, :, :, :]
            nc.vector.tensor_tensor(out=factor, in0=factor, in1=st, op=ALU.mult)

        def round_dz(h, j):
            if j == 0:
                dz.append(slot("dz%d" % h, UNIT, BF16))
            cols = slice(j * D, (j + 1) * D)
            nc.vector.scalar_tensor_tensor(out=dz[h][:, cols], in0=dh[h, j][:], scalar=-1.0, in1=gate[h][:, cols],
                                           op0=ALU.mult, op1=ALU.mult)

        def transpose_unit(words, banks, columns):
            unit = unit_tile()
            dst = unit[:].bitcast(F32).rearrange("q (%s u) -> q j p u" % columns, j=PACK, u=2)
            for b in range(2):
                turned = bank(banks[b])
                for r in range(2):
                    for u in range(2):
                        k = 2 * r + u
                        nc.tensor.transpose(turned[:, k * P:(k + 1) * P], words[:, 2 * b + r, u:2 * P:2], ident[:])
                walk = "q j p u -> q %s u" % columns
                nc.scalar.copy(out=dst[:, 2 * b:2 * b + 2, :, :].rearrange(walk),
                               in_=turned[:].rearrange("q (j u p) -> q j p u", j=2, u=2).rearrange(walk))
            return unit

        w_mx, dzf_mx, dzn_mx, x_mx = {}, {}, {}, {}

        def turn_w(g, banks):
            units["w", g] = transpose_unit(w_words[g], banks, "p j")

        def quant_w(g):
            w_mx[g] = quantize(units["w", g], W_SLOT + g, E4M3)

        def turn_dz(h, banks):
            units["dzf", h] = transpose_unit(dz[h][:].bitcast(F32).rearrange("p (j x) -> p j x", j=PACK), banks, "j p")

        def quant_dzf(h):
            dzf_mx[h] = quantize(units["dzf", h], G_SLOT + h, E5M2)

        def copy_dzn(h):
            units["dzn", h] = interleave(True, dz[h][:].rearrange("p (j w) -> p j w", j=PACK))

        def quant_dzn(h):
            dzn_mx[h] = quantize(units["dzn", h], G_SLOT + HALVES + h, E5M2)

        def copy_x(c, h):
            units["x", c, h] = interleave(True, x_rows[h][:, :, c * KP:(c + 1) * KP])

        def quant_x(c, h):
            index = HALVES * c + h
            x_mx[c, h] = quantize(units["x", c, h], A_SLOT + index if index < G_SLOT else X_EXTRA_SLOT + h, E4M3)

        def out0_chunk(g, result, banks):
            for j in range(PACK):
                acc = bank(banks[j])
                multiply(acc, dzf_mx[0], j, w_mx[g], True, True)
                nc.scalar.copy(out=result[:, j, :], in_=acc[:])

        def result_rows(tag, chunks):
            tile = slot(tag, chunks * UNIT, F32)
            return tile[:].rearrange("p (j w) -> p j w", j=PACK)

        def store_out0_chunks(first, result):
            nc.sync.dma_start(out=by_node(out_0[0, :, first * KP:first * KP + result.shape[2]], 0), in_=result)

        def out0_tile(j, tag, banks):
            result = slot(tag, F, F32)
            for g in range(CHUNKS):
                acc = bank(banks[(CHUNKS * j + g) % BANKS])
                multiply(acc, dzf_mx[1], j, w_mx[g], True, True)
                nc.scalar.copy(out=result[:, g * KP:(g + 1) * KP], in_=acc[:])
            nc.sync.dma_start(out=by_node(out_0[0, :, :], 1)[:, j, :], in_=result[:])

        def out1_chunk(c, tag, shared):
            result = slot(tag, UNIT, F32)
            for i in range(PACK):
                acc = bank((PACK * c + i) % BANKS)
                for h in range(HALVES):
                    multiply(acc, x_mx[c, h], i, dzn_mx[h], h == 0, h == HALVES - 1)
                copy(shared and i % 2 == 1, result[:, i * D:(i + 1) * D], acc[:])
            nc.sync.dma_start(out=out_1[c * KP:(c + 1) * KP, :].rearrange("(i p) n -> p i n", p=P),
                              in_=result[:].rearrange("p (i n) -> p i n", i=PACK))

        empty_product(0)
        empty_product(1)
        gate_slope(0)
        times_state(0)
        for j0 in (0, 2):
            for j in (j0, j0 + 1):
                turn_product(0, j, j)
            for j in (j0, j0 + 1):
                add_direct(0, j)
        for j in range(PACK):
            round_dz(0, j)

        w_banks, out_banks = (4, 5), (2, 3, 6, 7)

        def sum_dh(j):
            turn_product(1, j, j % 2)
            add_direct(1, j)

        turn_w(0, w_banks)
        sum_dh(0)
        quant_w(0)
        turn_dz(0, (6, 7))
        turn_w(1, w_banks)
        quant_dzf(0)
        gate_slope(1)

        pair = result_rows("big", 2)
        out0_chunk(0, pair[:, :, :KP], out_banks)
        quant_w(1)
        times_state(1)
        sum_dh(1)
        turn_w(2, w_banks)

        out0_chunk(1, pair[:, :, KP:], out_banks)
        store_out0_chunks(0, pair)
        round_dz(1, 0)
        round_dz(1, 1)
        quant_w(2)
        sum_dh(2)
        turn_w(3, w_banks)
        copy_dzn(0)

        single = result_rows("stage0", 1)
        out0_chunk(2, single, out_banks)
        store_out0_chunks(2, single)
        round_dz(1, 2)
        quant_w(3)
        sum_dh(3)
        turn_w(4, w_banks)
        quant_dzn(0)
        copy_x(0, 0)
        round_dz(1, 3)

        single = result_rows("stage2", 1)
        out0_chunk(3, single, out_banks)
        store_out0_chunks(3, single)
        quant_w(4)
        turn_dz(1, w_banks)
        copy_dzn(1)
        quant_x(0, 0)

        single = result_rows("stage4", 1)
        out0_chunk(4, single, out_banks)
        store_out0_chunks(4, single)
        quant_dzf(1)
        quant_dzn(1)

        for j, tag in enumerate(("stage1", "stage3", "weight", "big")):
            out0_tile(j, tag, out_banks + w_banks + (0, 1))

        order = [(c, h) for c in range(CHUNKS) for h in range(HALVES)]
        copy_x(*order[1])
        for i in range(1, len(order)):
            if i + 1 < len(order):
                copy_x(*order[i + 1])
            quant_x(*order[i])

        for c, tag in enumerate(("stage0", "stage2", "stage4", "stage1", "stage3")):
            out1_chunk(c, tag, c >= CHUNKS - 2)
